import numpy as np
import ml_dtypes


def mxq(x, axis, fmt="e4m3"):
    dtype, down = {"e4m3": (ml_dtypes.float8_e4m3fn, 7), "e5m2": (ml_dtypes.float8_e5m2, 14)}[fmt]
    v = np.moveaxis(np.asarray(x, np.float32).astype(ml_dtypes.bfloat16).astype(np.float64), axis, -1)
    blocks = v.reshape(v.shape[:-1] + (-1, 32))
    amax = np.abs(blocks).max(-1, keepdims=True)
    byte = np.maximum(np.where(amax > 0, np.frexp(amax)[1] - 1 + 127, 0) - down, 1)
    scale = np.exp2(byte - 127.0)
    codes = (blocks / scale).astype(np.float32).astype(dtype).astype(np.float64)
    return np.moveaxis((codes * scale).reshape(v.shape), -1, axis)


WIDE = False


def mx_kscale(k):
    if not WIDE:
        return np.ones(k)
    levels = np.array([10, -10, 5, -5, 0])
    a = np.random.permutation(np.resize(levels, k // 512 * 4)).reshape(k // 512, 4)
    idx = np.arange(k)
    return np.exp2(a[idx // 512, idx % 128 // 32])


BF16 = ml_dtypes.bfloat16


def bf(x):
    return np.asarray(x, np.float32).astype(BF16)


def f64(x):
    return np.asarray(x).astype(np.float64)


B, A, S, F = 4096, 3, 128, 512


def setup_inputs():
    s, u = mx_kscale(F), mx_kscale(F)
    t, v = mx_kscale(F), mx_kscale(F)
    return {
        "h1": bf(np.maximum(np.random.standard_normal((B, A, F)) * 1.4, 0.0) * s),
        "W2": bf(np.random.standard_normal((A, F, F)) * 1.4 / np.sqrt(F) / s[:, None] * t),
        "b2": bf(np.random.standard_normal((A, F)) * 0.2 * t),
        "W3": bf(np.random.standard_normal((A, F, S)) / np.sqrt(F) / t[:, None]),
        "b3": bf(np.random.standard_normal((A, S)) * 0.2),
        "g1": bf(np.maximum(np.random.standard_normal((B, F)) * 1.4, 0.0) * u),
        "V2": bf(np.random.standard_normal((F, F)) * 1.4 / np.sqrt(F) / u[:, None] * v),
        "c2": bf(np.random.standard_normal(F) * 0.2 * v),
        "V3": bf(np.random.standard_normal((F, S)) / np.sqrt(F) / v[:, None]),
        "c3": bf(np.random.standard_normal(S) * 0.2),
    }


def reference(h1, W2, b2, W3, b3, g1, V2, c2, V3, c3):
    ha = mxq(f64(h1), 2, "e4m3").transpose(1, 0, 2)
    h2 = np.maximum((ha @ mxq(f64(W2), 1, "e4m3")) + f64(b2)[:, None, :], 0.0)
    psi_adv = ((mxq(h2, 2, "e4m3") @ mxq(f64(W3), 1, "e4m3")) + f64(b3)[:, None, :]).transpose(1, 0, 2)
    g2 = np.maximum((mxq(f64(g1), 1, "e4m3") @ mxq(f64(V2), 0, "e4m3")) + f64(c2), 0.0)
    psi_state = (mxq(g2, 1, "e4m3") @ mxq(f64(V3), 0, "e4m3")) + f64(c3)
    return psi_state[:, None, :] + psi_adv - psi_adv.mean(axis=1, keepdims=True)

@@ -1,0 +1,341 @@
+from contextlib import ExitStack
+
+import concourse.mybir as mybir
+from concourse.masks import make_identity
+
+F32 = mybir.dt.float32
+BF16 = mybir.dt.bfloat16
+U32 = mybir.dt.uint32
+U8 = mybir.dt.uint8
+FP8X4 = mybir.dt.float8_e4m3fn_x4
+ACT = mybir.ActivationFunctionType
+ALU = mybir.AluOpType
+
+P = 128
+B, A, S, F = 4096, 3, 128, 512
+NS = A + 1
+ROUND = 512
+NR = B // ROUND
+NU = NR * NS
+ORDER = (3, 0, 1, 2)
+FLOPS = 2 * NS * B * (F * F + F * S)
+
+MANUAL = True
+LA = 3
+LB = 2
+LC = 1
+
+
+def tile_psicritic_pa_t_kernel(tc, h1, W2, b2, W3, b3, g1, V2, c2, V3, c3, out):
+    nc = tc.nc
+    with ExitStack() as ctx:
+        if MANUAL:
+            ctx.enter_context(tc.manual_schedule())
+        const = ctx.enter_context(tc.tile_pool(name="const", bufs=1))
+        wst = ctx.enter_context(tc.tile_pool(name="wst", bufs=2))
+        xin = ctx.enter_context(tc.tile_pool(name="xin", bufs=3))
+        xqp = ctx.enter_context(tc.tile_pool(name="xqp", bufs=3))
+        hpp = ctx.enter_context(tc.tile_pool(name="hpp", bufs=3))
+        hcp = ctx.enter_context(tc.tile_pool(name="hcp", bufs=2))
+        outp = ctx.enter_context(tc.tile_pool(name="outp", bufs=2))
+        ps_x = ctx.enter_context(tc.psum_pool(name="ps_x", bufs=2))
+        ps_h = ctx.enter_context(tc.psum_pool(name="ps_h", bufs=4))
+        ps_o = ctx.enter_context(tc.psum_pool(name="ps_o", bufs=2))
+
+        ident = const.tile([P, P], F32, name="ident")
+        make_identity(nc, ident[:])
+        ones = const.tile([P, P], BF16, name="ones")
+        nc.vector.memset(ones[:], 1.0)
+        bz = const.tile([P, P], BF16, name="bz")
+        nc.vector.memset(bz[:], 0.0)
+        zrow = const.tile([P, 4 * S], BF16, name="zrow")
+        nc.vector.memset(zrow[:], 0.0)
+
+        w2c = const.tile([P, NS * F], U32, name="w2c", align_bytes=64)
+        w2s = const.tile([P, NS * F], U8, name="w2s", align_bytes=64)
+        w3c = const.tile([P, NS * S], U32, name="w3c", align_bytes=64)
+        w3s = const.tile([P, NS * S], U8, name="w3s", align_bytes=64)
+        bias2 = const.tile([P, 4 * NS], F32, name="bias2")
+        beta = const.tile([P, A * S], F32, name="beta")
+
+        xh = {}
+        xg = {}
+
+        def load_g(r):
+            xg[r] = xin.tile([P, 4 * F], BF16, name="xg", tag="xg")
+            nc.sync.dma_start(
+                out=xg[r][:],
+                in_=g1[ROUND * r : ROUND * (r + 1), :].rearrange("(p j) k -> p (j k)", j=4),
+            )
+
+        def load_h(r, whole):
+            xh[r] = xin.tile([P, 4 * A * F], BF16, name="xh", tag="xh")
+            rows = h1[ROUND * r : ROUND * (r + 1)]
+            if whole:
+                nc.sync.dma_start(out=xh[r][:], in_=rows.rearrange("(p j) a k -> p (j a k)", j=4))
+
+        def load_h_part(r, a):
+            rows = h1[ROUND * r : ROUND * (r + 1), a : a + 1, :]
+            nc.sync.dma_start(
+                out=xh[r][:].rearrange("p (j a k) -> p j a k", j=4, a=A)[:, :, a : a + 1, :],
+                in_=rows.rearrange("(p j) o k -> p j o k", j=4),
+            )
+
+        w2raw = {}
+
+        def load_w2(s):
+            w2raw[s] = wst.tile([P, 4 * F], BF16, name="w2raw", tag="w2raw", bufs=4)
+            src = V2.rearrange("(u p e) n -> p u (e n)", u=2, e=2) if s == 3 else W2[
+                s : s + 1
+            ].rearrange("o (u p e) n -> p (o u) (e n)", u=2, e=2)
+            nc.sync.dma_start(out=w2raw[s][:].rearrange("p (u x) -> p u x", u=2), in_=src)
+
+        def prep_w2(s):
+            wg = wst.tile([P, 4 * F], BF16, name="wg", tag="wg", align_bytes=64)
+            nc.vector.tensor_copy(
+                out=wg[:].rearrange("p (c i t) -> p c t i", i=4, t=4),
+                in_=w2raw[s][:].rearrange("p (t c i) -> p c t i", t=4, i=4),
+            )
+            return wg
+
+        def quant_w2(s, wg):
+            nc.vector.quantize_mx(
+                out=w2c[:, F * s : F * (s + 1)].bitcast(FP8X4),
+                scales=w2s[:, F * s : F * (s + 1)],
+                in_=wg[:],
+            )
+
+        load_g(0)
+        load_w2(3)
+        nc.scalar.dma_start(out=bz[0 : 4 * A, :], in_=b2.rearrange("a (t p) -> (a t) p", p=P))
+        nc.scalar.dma_start(out=bz[4 * A : 4 * NS, :], in_=c2.rearrange("(t p) -> t p", p=P))
+        nc.scalar.dma_start(out=zrow[0:1, 0 : A * S], in_=b3.rearrange("(o a) s -> o (a s)", o=1))
+        nc.scalar.dma_start(out=zrow[0:1, A * S :], in_=c3.rearrange("(o s) -> o s", o=1))
+        load_h(0, False)
+        for a in range(A):
+            load_h_part(0, a)
+            load_w2(a)
+        w3raw = const.tile([P, NS * 4 * S], BF16, name="w3raw")
+        nc.sync.dma_start(
+            out=w3raw[:, 0 : A * 4 * S].rearrange("p (x n) -> p x n", n=S),
+            in_=W3.rearrange("a (t p) n -> p (a t) n", p=P),
+        )
+        nc.sync.dma_start(
+            out=w3raw[:, A * 4 * S :].rearrange("p (x n) -> p x n", n=S),
+            in_=V3.rearrange("(t p) n -> p t n", p=P),
+        )
+        for r in (1, 2):
+            load_g(r)
+            load_h(r, True)
+
+        xt = {}
+        xq = {}
+        xc = {}
+        hps = {}
+        hp = {}
+        hq = {}
+        hc = {}
+        ops = {}
+        osb = {}
+        esb = {}
+
+        def unit(u):
+            return u // NS, ORDER[u % NS]
+
+        def st_a(u, hf):
+            r, s = unit(u)
+            x32 = (xg[r] if s == 3 else xh[r])[:].bitcast(F32)
+            xt[u, hf] = ps_x.tile([P, 512], F32, name="xt", tag="xt")
+            for uu in range(2):
+                for jj in range(2):
+                    j = 2 * hf + jj
+                    col = (j * 256 if s == 3 else (j * A + s) * 256) + 128 * uu
+                    nc.tensor.transpose(
+                        xt[u, hf][:, (2 * uu + jj) * P : (2 * uu + jj + 1) * P],
+                        x32[:, col : col + P],
+                        ident[:],
+                    )
+
+        def st_b(u, hf):
+            if hf == 0:
+                xq[u] = xqp.tile([P, 4 * ROUND], BF16, name="xq", tag="xq", align_bytes=64)
+            dst = xq[u][:].bitcast(F32).rearrange("p (w u) -> p w u", u=2)
+            nc.scalar.copy(
+                out=dst[:, 256 * hf : 256 * (hf + 1), :],
+                in_=xt[u, hf][:].rearrange("p (u w) -> p w u", u=2),
+            )
+
+        def st_c(u):
+            codes = xqp.tile([P, ROUND], U32, name="xc", tag="xc", align_bytes=64)
+            scales = xqp.tile([P, ROUND], U8, name="xs", tag="xs", align_bytes=64)
+            xc[u] = (codes, scales)
+            nc.vector.quantize_mx(out=codes[:].bitcast(FP8X4), scales=scales[:], in_=xq[u][:])
+
+        def st_d(u, t):
+            r, s = unit(u)
+            hps[u, t] = ps_h.tile([P, ROUND], F32, name="hps", tag="hps")
+            col = F * s + P * t
+            nc.tensor.matmul_mx(
+                out=hps[u, t][:],
+                lhsT=w2c[:, col : col + P].bitcast(FP8X4),
+                lhsT_scale=w2s[:, col : col + P],
+                rhs=xc[u][0][:].bitcast(FP8X4),
+                rhs_scale=xc[u][1][:],
+                start=True,
+                stop=True,
+            )
+
+        def st_e(u, t):
+            r, s = unit(u)
+            if t == 0:
+                hp[u] = hpp.tile([P, 4 * ROUND], BF16, name="hp", tag="hp")
+            nc.scalar.activation(
+                out=hp[u][:, ROUND * t : ROUND * (t + 1)],
+                in_=hps[u, t][:],
+                func=ACT.Relu,
+                bias=bias2[:, 4 * s + t : 4 * s + t + 1],
+                scale=1.0,
+            )
+
+        def st_f(u):
+            hq[u] = hpp.tile([P, 4 * ROUND], BF16, name="hq", tag="hq", align_bytes=64)
+            nc.vector.tensor_copy(
+                out=hq[u][:].rearrange("p (c i t) -> p c t i", i=4, t=4),
+                in_=hp[u][:].rearrange("p (t c i) -> p c t i", t=4, i=4),
+            )
+
+        def st_g(u):
+            r, s = unit(u)
+            codes = hcp.tile([P, ROUND], U32, name="hc%d" % s, tag="hc%d" % s, align_bytes=64)
+            scales = hcp.tile([P, ROUND], U8, name="hs%d" % s, tag="hs%d" % s, align_bytes=64)
+            hc[r, s] = (codes, scales)
+            nc.vector.quantize_mx(out=codes[:].bitcast(FP8X4), scales=scales[:], in_=hq[u][:])
+
+        def l2_pass(dst, r, s, j, start, stop):
+            nc.tensor.matmul_mx(
+                out=dst,
+                lhsT=hc[r, s][0][:, P * j : P * (j + 1)].bitcast(FP8X4),
+                lhsT_scale=hc[r, s][1][:, P * j : P * (j + 1)],
+                rhs=w3c[:, S * s : S * (s + 1)].bitcast(FP8X4),
+                rhs_scale=w3s[:, S * s : S * (s + 1)],
+                start=start,
+                stop=stop,
+            )
+
+        def st_h(r, j):
+            ops[r, j] = ps_o.tile([P, 4 * S], F32, name="ops", tag="ops")
+            for a in range(A):
+                dst = ops[r, j][:, S * a : S * (a + 1)]
+                l2_pass(dst, r, 3, j, True, False)
+                l2_pass(dst, r, a, j, False, True)
+            for a in range(A):
+                l2_pass(ops[r, j][:, S * A :], r, a, j, a == 0, a == A - 1)
+
+        def st_i1(r, j):
+            esb[r, j] = outp.tile([P, A * S], F32, name="esb", tag="esb")
+            nc.vector.scalar_tensor_tensor(
+                out=esb[r, j][:].rearrange("p (a s) -> p a s", a=A),
+                in0=ops[r, j][:, S * A :].unsqueeze(1).to_broadcast([P, A, S]),
+                scalar=-1.0 / 3.0,
+                in1=beta[:].rearrange("p (a s) -> p a s", a=A),
+                op0=ALU.mult,
+                op1=ALU.add,
+            )
+
+        def st_i2(r, j):
+            if j == 0:
+                osb[r] = outp.tile([P, 4 * A * S], F32, name="osb", tag="osb")
+            nc.vector.tensor_tensor(
+                out=osb[r][:, A * S * j : A * S * (j + 1)],
+                in0=ops[r, j][:, 0 : A * S],
+                in1=esb[r, j][:],
+                op=ALU.add,
+            )
+            if j == 3:
+                nc.sync.dma_start(
+                    out=out[ROUND * r : ROUND * (r + 1)].rearrange("(p j) a s -> p (j a s)", j=4),
+                    in_=osb[r][:],
+                )
+
+        def setup_bias2():
+            bz32 = const.tile([P, P], F32, name="bz32")
+            nc.vector.tensor_copy(out=bz32[:], in_=bz[:])
+            pt = ps_o.tile([P, 4 * S], F32, name="pt", tag="ops")
+            nc.tensor.transpose(pt[:, 0:P], bz32[:], ident[:])
+            wg = prep_w2(3)
+            nc.vector.tensor_copy(out=bias2[:], in_=pt[:, 0 : 4 * NS])
+            quant_w2(3, wg)
+
+        def setup_beta():
+            pb = ps_o.tile([P, 4 * S], F32, name="pb", tag="ops")
+            nc.tensor.matmul(out=pb[:], lhsT=ones[:], rhs=zrow[:], start=True, stop=True)
+            bb = const.tile([P, 4 * S], F32, name="bb")
+            nc.vector.tensor_copy(out=bb[:], in_=pb[:])
+            m1 = const.tile([P, S], F32, name="m1")
+            nc.vector.tensor_tensor(out=m1[:], in0=bb[:, 0:S], in1=bb[:, S : 2 * S], op=ALU.add)
+            m2 = const.tile([P, S], F32, name="m2")
+            nc.vector.tensor_tensor(out=m2[:], in0=m1[:], in1=bb[:, 2 * S : 3 * S], op=ALU.add)
+            gm = const.tile([P, S], F32, name="gm")
+            nc.vector.scalar_tensor_tensor(
+                out=gm[:], in0=m2[:], scalar=-1.0 / 3.0, in1=bb[:, 3 * S :], op0=ALU.mult, op1=ALU.add
+            )
+            nc.vector.tensor_tensor(
+                out=beta[:].rearrange("p (a s) -> p a s", a=A),
+                in0=bb[:, 0 : A * S].rearrange("p (a s) -> p a s", a=A),
+                in1=gm[:].unsqueeze(1).to_broadcast([P, A, S]),
+                op=ALU.add,
+            )
+
+        def setup_w3():
+            w3g = const.tile([P, NS * 4 * S], BF16, name="w3g", align_bytes=64)
+            nc.vector.tensor_copy(
+                out=w3g[:].rearrange("p (s n t) -> p s n t", s=NS, t=4),
+                in_=w3raw[:].rearrange("p (s t n) -> p s n t", s=NS, t=4),
+            )
+            return w3g
+
+        pending = {}
+        for n in range(-LA, NU + 6):
+            if n >= 2 and n % NS == 2 and n // NS + 3 < NR:
+                load_g(n // NS + 3)
+                load_h(n // NS + 3, True)
+            if 0 <= n + LC < NU:
+                st_c(n + LC)
+            if n == -1:
+                pending[0] = prep_w2(0)
+            if n == 0:
+                quant_w2(0, pending[0])
+                pending[1] = prep_w2(1)
+            if n == 1:
+                quant_w2(1, pending[1])
+                pending[2] = prep_w2(2)
+            if n == 2:
+                quant_w2(2, pending[2])
+                pending[3] = setup_w3()
+                setup_beta()
+            if n == 3:
+                nc.vector.quantize_mx(out=w3c[:].bitcast(FP8X4), scales=w3s[:], in_=pending[3][:])
+            for t in range(4):
+                if 0 <= n < NU:
+                    st_e(n, t)
+                if 0 <= n + 1 < NU:
+                    st_d(n + 1, t)
+            m = n - 5
+            if 0 <= m < NU:
+                st_h(m // 4, m % 4)
+            for hf in range(2):
+                if 0 <= n + LB < NU:
+                    st_b(n + LB, hf)
+                if 0 <= n + LA < NU:
+                    st_a(n + LA, hf)
+            if n == -LA:
+                setup_bias2()
+            m = n - 6
+            if 0 <= n - 1 < NU:
+                st_f(n - 1)
+            if 0 <= m < NU:
+                st_i1(m // 4, m % 4)
+            if 0 <= n - 1 < NU:
+                st_g(n - 1)
+            if 0 <= m < NU:
+                st_i2(m // 4, m % 4)

@@ -21,9 +21,9 @@ ORDER = (3, 0, 1, 2)
 FLOPS = 2 * NS * B * (F * F + F * S)
 
 MANUAL = True
-LA = 3
-LB = 2
-LC = 1
+LEAD_B = 3
+LEAD_C = 2
+FULL_ROUNDS = 7
 
 
 def tile_psicritic_pa_t_kernel(tc, h1, W2, b2, W3, b3, g1, V2, c2, V3, c3, out):
@@ -34,7 +34,7 @@ def tile_psicritic_pa_t_kernel(tc, h1, W2, b2, W3, b3, g1, V2, c2, V3, c3, out):
         const = ctx.enter_context(tc.tile_pool(name="const", bufs=1))
         wst = ctx.enter_context(tc.tile_pool(name="wst", bufs=2))
         xin = ctx.enter_context(tc.tile_pool(name="xin", bufs=3))
-        xqp = ctx.enter_context(tc.tile_pool(name="xqp", bufs=3))
+        xqp = ctx.enter_context(tc.tile_pool(name="xqp", bufs=4))
         hpp = ctx.enter_context(tc.tile_pool(name="hpp", bufs=3))
         hcp = ctx.enter_context(tc.tile_pool(name="hcp", bufs=2))
         outp = ctx.enter_context(tc.tile_pool(name="outp", bufs=2))
@@ -53,8 +53,8 @@ def tile_psicritic_pa_t_kernel(tc, h1, W2, b2, W3, b3, g1, V2, c2, V3, c3, out):
 
         w2c = const.tile([P, NS * F], U32, name="w2c", align_bytes=64)
         w2s = const.tile([P, NS * F], U8, name="w2s", align_bytes=64)
-        w3c = const.tile([P, NS * S], U32, name="w3c", align_bytes=64)
-        w3s = const.tile([P, NS * S], U8, name="w3s", align_bytes=64)
+        w3c = const.tile([P, 8 * S], U32, name="w3c", align_bytes=64)
+        w3s = const.tile([P, 8 * S], U8, name="w3s", align_bytes=64)
         bias2 = const.tile([P, 4 * NS], F32, name="bias2")
         beta = const.tile([P, A * S], F32, name="beta")
 
@@ -90,12 +90,14 @@ def tile_psicritic_pa_t_kernel(tc, h1, W2, b2, W3, b3, g1, V2, c2, V3, c3, out):
             ].rearrange("o (u p e) n -> p (o u) (e n)", u=2, e=2)
             nc.sync.dma_start(out=w2raw[s][:].rearrange("p (u x) -> p u x", u=2), in_=src)
 
-        def prep_w2(s):
+        def prep_w2(s, on_gpsimd=False):
             wg = wst.tile([P, 4 * F], BF16, name="wg", tag="wg", align_bytes=64)
-            nc.vector.tensor_copy(
-                out=wg[:].rearrange("p (c i t) -> p c t i", i=4, t=4),
-                in_=w2raw[s][:].rearrange("p (t c i) -> p c t i", t=4, i=4),
-            )
+            dst = wg[:].rearrange("p (c i t) -> p c t i", i=4, t=4)
+            src = w2raw[s][:].rearrange("p (t c i) -> p c t i", t=4, i=4)
+            if on_gpsimd:
+                nc.gpsimd.tensor_scalar(out=dst, in0=src, scalar1=1.0, scalar2=0.0, op0=ALU.mult, op1=ALU.add)
+            else:
+                nc.vector.tensor_copy(out=dst, in_=src)
             return wg
 
         def quant_w2(s, wg):
@@ -142,6 +144,9 @@ def tile_psicritic_pa_t_kernel(tc, h1, W2, b2, W3, b3, g1, V2, c2, V3, c3, out):
         def unit(u):
             return u // NS, ORDER[u % NS]
 
+        def b_on_vector(u, hf):
+            return hf == 1 and u >= 2 and u % 2 == 0
+
         def st_a(u, hf):
             r, s = unit(u)
             x32 = (xg[r] if s == 3 else xh[r])[:].bitcast(F32)
@@ -159,11 +164,12 @@ def tile_psicritic_pa_t_kernel(tc, h1, W2, b2, W3, b3, g1, V2, c2, V3, c3, out):
         def st_b(u, hf):
             if hf == 0:
                 xq[u] = xqp.tile([P, 4 * ROUND], BF16, name="xq", tag="xq", align_bytes=64)
-            dst = xq[u][:].bitcast(F32).rearrange("p (w u) -> p w u", u=2)
-            nc.scalar.copy(
-                out=dst[:, 256 * hf : 256 * (hf + 1), :],
-                in_=xt[u, hf][:].rearrange("p (u w) -> p w u", u=2),
-            )
+            dst = xq[u][:].bitcast(F32).rearrange("p (w u) -> p w u", u=2)[:, 256 * hf : 256 * (hf + 1), :]
+            src = xt[u, hf][:].rearrange("p (u w) -> p w u", u=2)
+            if b_on_vector(u, hf):
+                nc.vector.tensor_copy(out=dst, in_=src)
+            else:
+                nc.scalar.copy(out=dst, in_=src)
 
         def st_c(u):
             codes = xqp.tile([P, ROUND], U32, name="xc", tag="xc", align_bytes=64)
@@ -211,13 +217,13 @@ def tile_psicritic_pa_t_kernel(tc, h1, W2, b2, W3, b3, g1, V2, c2, V3, c3, out):
             hc[r, s] = (codes, scales)
             nc.vector.quantize_mx(out=codes[:].bitcast(FP8X4), scales=scales[:], in_=hq[u][:])
 
-        def l2_pass(dst, r, s, j, start, stop):
+        def l2_pass(dst, r, s, j, blk, start, stop):
             nc.tensor.matmul_mx(
                 out=dst,
                 lhsT=hc[r, s][0][:, P * j : P * (j + 1)].bitcast(FP8X4),
                 lhsT_scale=hc[r, s][1][:, P * j : P * (j + 1)],
-                rhs=w3c[:, S * s : S * (s + 1)].bitcast(FP8X4),
-                rhs_scale=w3s[:, S * s : S * (s + 1)],
+                rhs=w3c[:, S * blk : S * (blk + 1)].bitcast(FP8X4),
+                rhs_scale=w3s[:, S * blk : S * (blk + 1)],
                 start=start,
                 stop=stop,
             )
@@ -226,17 +232,26 @@ def tile_psicritic_pa_t_kernel(tc, h1, W2, b2, W3, b3, g1, V2, c2, V3, c3, out):
             ops[r, j] = ps_o.tile([P, 4 * S], F32, name="ops", tag="ops")
             for a in range(A):
                 dst = ops[r, j][:, S * a : S * (a + 1)]
-                l2_pass(dst, r, 3, j, True, False)
-                l2_pass(dst, r, a, j, False, True)
-            for a in range(A):
-                l2_pass(ops[r, j][:, S * A :], r, a, j, a == 0, a == A - 1)
+                if r < FULL_ROUNDS:
+                    l2_pass(dst, r, 3, j, 3, True, False)
+                    l2_pass(dst, r, 3, j, 7, False, False)
+                    for b in range(A):
+                        l2_pass(dst, r, b, j, b if b == a else 4 + b, False, b == A - 1)
+                else:
+                    l2_pass(dst, r, 3, j, 3, True, False)
+                    l2_pass(dst, r, a, j, a, False, True)
+            if r >= FULL_ROUNDS:
+                for a in range(A):
+                    l2_pass(ops[r, j][:, S * A :], r, a, j, 4 + a, a == 0, a == A - 1)
 
         def st_i1(r, j):
+            if r < FULL_ROUNDS:
+                return
             esb[r, j] = outp.tile([P, A * S], F32, name="esb", tag="esb")
             nc.vector.scalar_tensor_tensor(
                 out=esb[r, j][:].rearrange("p (a s) -> p a s", a=A),
                 in0=ops[r, j][:, S * A :].unsqueeze(1).to_broadcast([P, A, S]),
-                scalar=-1.0 / 3.0,
+                scalar=1.0 / 3.0,
                 in1=beta[:].rearrange("p (a s) -> p a s", a=A),
                 op0=ALU.mult,
                 op1=ALU.add,
@@ -245,17 +260,23 @@ def tile_psicritic_pa_t_kernel(tc, h1, W2, b2, W3, b3, g1, V2, c2, V3, c3, out):
         def st_i2(r, j):
             if j == 0:
                 osb[r] = outp.tile([P, 4 * A * S], F32, name="osb", tag="osb")
-            nc.vector.tensor_tensor(
+            full = r < FULL_ROUNDS
+            nc.vector.scalar_tensor_tensor(
                 out=osb[r][:, A * S * j : A * S * (j + 1)],
                 in0=ops[r, j][:, 0 : A * S],
-                in1=esb[r, j][:],
-                op=ALU.add,
+                scalar=1.0 / 3.0 if full else 0.5,
+                in1=beta[:] if full else esb[r, j][:],
+                op0=ALU.mult,
+                op1=ALU.add,
             )
-            if j == 3:
+            rows = out[ROUND * r : ROUND * (r + 1)]
+            if r == NR - 1:
                 nc.sync.dma_start(
-                    out=out[ROUND * r : ROUND * (r + 1)].rearrange("(p j) a s -> p (j a s)", j=4),
-                    in_=osb[r][:],
+                    out=rows.rearrange("(p j) a s -> p j (a s)", j=4)[:, j : j + 1, :],
+                    in_=osb[r][:, A * S * j : A * S * (j + 1)].unsqueeze(1),
                 )
+            elif j == 3:
+                nc.sync.dma_start(out=rows.rearrange("(p j) a s -> p (j a s)", j=4), in_=osb[r][:])
 
         def setup_bias2():
             bz32 = const.tile([P, P], F32, name="bz32")
@@ -287,55 +308,115 @@ def tile_psicritic_pa_t_kernel(tc, h1, W2, b2, W3, b3, g1, V2, c2, V3, c3, out):
             )
 
         def setup_w3():
-            w3g = const.tile([P, NS * 4 * S], BF16, name="w3g", align_bytes=64)
-            nc.vector.tensor_copy(
-                out=w3g[:].rearrange("p (s n t) -> p s n t", s=NS, t=4),
-                in_=w3raw[:].rearrange("p (s t n) -> p s n t", s=NS, t=4),
-            )
+            w3g = const.tile([P, 8 * 4 * S], BF16, name="w3g", align_bytes=64)
+            for lo, hi, src_lo, factor in ((0, 4, 0, 2.0), (4, 7, 0, -1.0), (7, 8, 3, 1.0)):
+                nc.gpsimd.tensor_scalar(
+                    out=w3g[:, 4 * S * lo : 4 * S * hi].rearrange("p (s n t) -> p s n t", s=hi - lo, t=4),
+                    in0=w3raw[:, 4 * S * src_lo : 4 * S * (src_lo + hi - lo)].rearrange(
+                        "p (s t n) -> p s n t", s=hi - lo, t=4
+                    ),
+                    scalar1=factor,
+                    scalar2=0.0,
+                    op0=ALU.mult,
+                    op1=ALU.add,
+                )
             return w3g
 
-        pending = {}
-        for n in range(-LA, NU + 6):
+        state = {"a": 0, "b": 0, "c": 0, "h": 0, "i": 0}
+        ready = []
+        h_done = []
+        seen = {}
+
+        def b_unit(u):
+            for hf in range(2):
+                st_b(u, hf)
+                if state["a"] < NU:
+                    st_a(state["a"], hf)
+            state["a"] += 1
+            state["b"] = u + 1
+
+        def quantise_h(u, n):
+            st_g(u)
+            r = u // NS
+            seen[r] = seen.get(r, 0) + 1
+            if seen[r] == NS:
+                for j in range(4):
+                    ready.append((r, j, n))
+
+        def try_h(n, force):
+            if state["h"] < len(ready) and (force or ready[state["h"]][2] <= n - 1):
+                r, j = ready[state["h"]][0:2]
+                state["h"] += 1
+                st_h(r, j)
+                h_done.append((r, j, n))
+
+        def pop_i(n, force):
+            if state["i"] < len(h_done) and (force or h_done[state["i"]][2] <= n - 1):
+                state["i"] += 1
+                return h_done[state["i"] - 1]
+            return None
+
+        st_a(0, 0)
+        st_a(0, 1)
+        state["a"] = 1
+        setup_bias2()
+        b_unit(0)
+        st_c(0)
+        state["c"] = 1
+        for t in range(4):
+            st_d(0, t)
+        pending = {0: prep_w2(0)}
+        b_unit(1)
+        for n in range(NU):
             if n >= 2 and n % NS == 2 and n // NS + 3 < NR:
                 load_g(n // NS + 3)
                 load_h(n // NS + 3, True)
-            if 0 <= n + LC < NU:
-                st_c(n + LC)
-            if n == -1:
-                pending[0] = prep_w2(0)
+            while state["c"] < NU and state["c"] <= n + LEAD_C and state["c"] < state["b"]:
+                st_c(state["c"])
+                state["c"] += 1
+                if n < 2:
+                    break
             if n == 0:
                 quant_w2(0, pending[0])
                 pending[1] = prep_w2(1)
             if n == 1:
                 quant_w2(1, pending[1])
-                pending[2] = prep_w2(2)
+                pending[2] = prep_w2(2, True)
             if n == 2:
                 quant_w2(2, pending[2])
                 pending[3] = setup_w3()
                 setup_beta()
-            if n == 3:
+            if n == 4:
                 nc.vector.quantize_mx(out=w3c[:].bitcast(FP8X4), scales=w3s[:], in_=pending[3][:])
+            chunk = pop_i(n, False)
             for t in range(4):
-                if 0 <= n < NU:
-                    st_e(n, t)
-                if 0 <= n + 1 < NU:
+                st_e(n, t)
+                if n + 1 < NU:
                     st_d(n + 1, t)
-            m = n - 5
-            if 0 <= m < NU:
-                st_h(m // 4, m % 4)
-            for hf in range(2):
-                if 0 <= n + LB < NU:
-                    st_b(n + LB, hf)
-                if 0 <= n + LA < NU:
-                    st_a(n + LA, hf)
-            if n == -LA:
-                setup_bias2()
-            m = n - 6
-            if 0 <= n - 1 < NU:
+            try_h(n, False)
+            if n >= 1:
                 st_f(n - 1)
-            if 0 <= m < NU:
-                st_i1(m // 4, m % 4)
-            if 0 <= n - 1 < NU:
-                st_g(n - 1)
-            if 0 <= m < NU:
-                st_i2(m // 4, m % 4)
+            count = 0
+            while state["b"] < NU and state["b"] <= n + (2 if n < 1 else LEAD_B) and count < 2:
+                b_unit(state["b"])
+                count += 1
+            if chunk:
+                st_i1(chunk[0], chunk[1])
+            if n >= 1:
+                quantise_h(n - 1, n)
+            if chunk:
+                st_i2(chunk[0], chunk[1])
+        st_f(NU - 1)
+        chunk = pop_i(NU, True)
+        if chunk:
+            st_i1(chunk[0], chunk[1])
+        quantise_h(NU - 1, NU)
+        if chunk:
+            st_i2(chunk[0], chunk[1])
+        while state["i"] < NR * 4:
+            try_h(NU, True)
+            try_h(NU, True)
+            while state["i"] < len(h_done):
+                chunk = pop_i(NU, True)
+                st_i1(chunk[0], chunk[1])
+                st_i2(chunk[0], chunk[1])

@@ -23,7 +23,8 @@ FLOPS = 2 * NS * B * (F * F + F * S)
 MANUAL = True
 LEAD_B = 3
 LEAD_C = 2
-FULL_ROUNDS = 7
+FULL_ROUNDS = 0
+G_COLS = 192
 
 
 def tile_psicritic_pa_t_kernel(tc, h1, W2, b2, W3, b3, g1, V2, c2, V3, c3, out):
@@ -56,6 +57,7 @@ def tile_psicritic_pa_t_kernel(tc, h1, W2, b2, W3, b3, g1, V2, c2, V3, c3, out):
         w3c = const.tile([P, 8 * S], U32, name="w3c", align_bytes=64)
         w3s = const.tile([P, 8 * S], U8, name="w3s", align_bytes=64)
         bias2 = const.tile([P, 4 * NS], F32, name="bias2")
+        junk = const.tile([P, 16], BF16, name="junk")
         beta = const.tile([P, A * S], F32, name="beta")
 
         xh = {}
@@ -205,10 +207,23 @@ def tile_psicritic_pa_t_kernel(tc, h1, W2, b2, W3, b3, g1, V2, c2, V3, c3, out):
 
         def st_f(u):
             hq[u] = hpp.tile([P, 4 * ROUND], BF16, name="hq", tag="hq", align_bytes=64)
+            gcols = G_COLS if NS <= u < NU - 1 else 0
+            cut = ROUND - gcols
+            planes = hp[u][:].rearrange("p (t w) -> p t w", t=4)
             nc.vector.tensor_copy(
-                out=hq[u][:].rearrange("p (c i t) -> p c t i", i=4, t=4),
-                in_=hp[u][:].rearrange("p (t c i) -> p c t i", t=4, i=4),
+                out=hq[u][:, 0 : 4 * cut].rearrange("p (c i t) -> p c t i", i=4, t=4),
+                in_=planes[:, :, 0:cut].rearrange("p t (c i) -> p c t i", i=4),
             )
+            if gcols:
+                nc.gpsimd.tensor_copy(out=junk[:, 0:1], in_=hq[u][:, 0:1])
+                nc.gpsimd.tensor_scalar(
+                    out=hq[u][:, 4 * cut :].rearrange("p (c i t) -> p c t i", i=4, t=4),
+                    in0=planes[:, :, cut:].rearrange("p t (c i) -> p c t i", i=4),
+                    scalar1=1.0,
+                    scalar2=0.0,
+                    op0=ALU.mult,
+                    op1=ALU.add,
+                )
 
         def st_g(u):
             r, s = unit(u)
@@ -367,7 +382,7 @@ def tile_psicritic_pa_t_kernel(tc, h1, W2, b2, W3, b3, g1, V2, c2, V3, c3, out):
             st_d(0, t)
         pending = {0: prep_w2(0)}
         b_unit(1)
-        for n in range(NU):
+        for n in range(NU + 2):
             if n >= 2 and n % NS == 2 and n // NS + 3 < NR:
                 load_g(n // NS + 3)
                 load_h(n // NS + 3, True)
@@ -381,38 +396,32 @@ def tile_psicritic_pa_t_kernel(tc, h1, W2, b2, W3, b3, g1, V2, c2, V3, c3, out):
                 pending[1] = prep_w2(1)
             if n == 1:
                 quant_w2(1, pending[1])
-                pending[2] = prep_w2(2, True)
+                pending[2] = prep_w2(2)
             if n == 2:
                 quant_w2(2, pending[2])
                 pending[3] = setup_w3()
                 setup_beta()
             if n == 4:
                 nc.vector.quantize_mx(out=w3c[:].bitcast(FP8X4), scales=w3s[:], in_=pending[3][:])
-            chunk = pop_i(n, False)
-            for t in range(4):
-                st_e(n, t)
-                if n + 1 < NU:
-                    st_d(n + 1, t)
-            try_h(n, False)
-            if n >= 1:
+            chunk = pop_i(n, n >= NU)
+            if n < NU:
+                for t in range(4):
+                    st_e(n, t)
+                    if n + 1 < NU:
+                        st_d(n + 1, t)
+            try_h(n, n >= NU)
+            if 2 <= n:
+                quantise_h(n - 2, n)
+            if 1 <= n <= NU:
                 st_f(n - 1)
+            if chunk:
+                st_i1(chunk[0], chunk[1])
             count = 0
             while state["b"] < NU and state["b"] <= n + (2 if n < 1 else LEAD_B) and count < 2:
                 b_unit(state["b"])
                 count += 1
             if chunk:
-                st_i1(chunk[0], chunk[1])
-            if n >= 1:
-                quantise_h(n - 1, n)
-            if chunk:
                 st_i2(chunk[0], chunk[1])
-        st_f(NU - 1)
-        chunk = pop_i(NU, True)
-        if chunk:
-            st_i1(chunk[0], chunk[1])
-        quantise_h(NU - 1, NU)
-        if chunk:
-            st_i2(chunk[0], chunk[1])
         while state["i"] < NR * 4:
             try_h(NU, True)
             try_h(NU, True)

@@ -14,24 +14,22 @@ ALU = mybir.AluOpType
 P = 128
 B, A, S, F = 4096, 3, 128, 512
 NS = A + 1
-ROUND = 512
-NR = B // ROUND
-NU = NR * NS
 ORDER = (3, 0, 1, 2)
+ROUNDS = (512, 512, 512, 512, 512, 512, 512, 256, 256)
+NR = len(ROUNDS)
+NU = NR * NS
 FLOPS = 2 * NS * B * (F * F + F * S)
 
-MANUAL = True
 LEAD_B = 3
 LEAD_C = 2
-FULL_ROUNDS = 0
-G_COLS = 192
+FULL = (0, 1, 2, 3, 4, 5, 6)
+V_SHARE = 6
 
 
 def tile_psicritic_pa_t_kernel(tc, h1, W2, b2, W3, b3, g1, V2, c2, V3, c3, out):
     nc = tc.nc
+    base = [sum(ROUNDS[:r]) for r in range(NR)]
     with ExitStack() as ctx:
-        if MANUAL:
-            ctx.enter_context(tc.manual_schedule())
         const = ctx.enter_context(tc.tile_pool(name="const", bufs=1))
         wst = ctx.enter_context(tc.tile_pool(name="wst", bufs=2))
         xin = ctx.enter_context(tc.tile_pool(name="xin", bufs=3))
@@ -57,30 +55,38 @@ def tile_psicritic_pa_t_kernel(tc, h1, W2, b2, W3, b3, g1, V2, c2, V3, c3, out):
         w3c = const.tile([P, 8 * S], U32, name="w3c", align_bytes=64)
         w3s = const.tile([P, 8 * S], U8, name="w3s", align_bytes=64)
         bias2 = const.tile([P, 4 * NS], F32, name="bias2")
-        junk = const.tile([P, 16], BF16, name="junk")
         beta = const.tile([P, A * S], F32, name="beta")
 
         xh = {}
         xg = {}
 
-        def load_g(r):
-            xg[r] = xin.tile([P, 4 * F], BF16, name="xg", tag="xg")
-            nc.sync.dma_start(
-                out=xg[r][:],
-                in_=g1[ROUND * r : ROUND * (r + 1), :].rearrange("(p j) k -> p (j k)", j=4),
-            )
+        def chunks(r):
+            return ROUNDS[r] // P
+
+        def load_g(r, parts=1):
+            nj = chunks(r)
+            xg[r] = xin.tile([P, nj * F], BF16, name="xg", tag="xg")
+            rows = g1[base[r] : base[r] + ROUNDS[r], :].rearrange("(p j) k -> p j k", j=nj)
+            step = nj // parts
+            for i in range(parts):
+                nc.sync.dma_start(
+                    out=xg[r][:, F * step * i : F * step * (i + 1)].rearrange("p (j k) -> p j k", k=F),
+                    in_=rows[:, step * i : step * (i + 1), :],
+                )
 
         def load_h(r, whole):
-            xh[r] = xin.tile([P, 4 * A * F], BF16, name="xh", tag="xh")
-            rows = h1[ROUND * r : ROUND * (r + 1)]
+            nj = chunks(r)
+            xh[r] = xin.tile([P, nj * A * F], BF16, name="xh", tag="xh")
             if whole:
-                nc.sync.dma_start(out=xh[r][:], in_=rows.rearrange("(p j) a k -> p (j a k)", j=4))
+                rows = h1[base[r] : base[r] + ROUNDS[r]]
+                nc.sync.dma_start(out=xh[r][:], in_=rows.rearrange("(p j) a k -> p (j a k)", j=nj))
 
         def load_h_part(r, a):
-            rows = h1[ROUND * r : ROUND * (r + 1), a : a + 1, :]
+            nj = chunks(r)
+            rows = h1[base[r] : base[r] + ROUNDS[r], a : a + 1, :]
             nc.sync.dma_start(
-                out=xh[r][:].rearrange("p (j a k) -> p j a k", j=4, a=A)[:, :, a : a + 1, :],
-                in_=rows.rearrange("(p j) o k -> p j o k", j=4),
+                out=xh[r][:].rearrange("p (j a k) -> p j a k", j=nj, a=A)[:, :, a : a + 1, :],
+                in_=rows.rearrange("(p j) o k -> p j o k", j=nj),
             )
 
         w2raw = {}
@@ -92,14 +98,12 @@ def tile_psicritic_pa_t_kernel(tc, h1, W2, b2, W3, b3, g1, V2, c2, V3, c3, out):
             ].rearrange("o (u p e) n -> p (o u) (e n)", u=2, e=2)
             nc.sync.dma_start(out=w2raw[s][:].rearrange("p (u x) -> p u x", u=2), in_=src)
 
-        def prep_w2(s, on_gpsimd=False):
+        def prep_w2(s):
             wg = wst.tile([P, 4 * F], BF16, name="wg", tag="wg", align_bytes=64)
-            dst = wg[:].rearrange("p (c i t) -> p c t i", i=4, t=4)
-            src = w2raw[s][:].rearrange("p (t c i) -> p c t i", t=4, i=4)
-            if on_gpsimd:
-                nc.gpsimd.tensor_scalar(out=dst, in0=src, scalar1=1.0, scalar2=0.0, op0=ALU.mult, op1=ALU.add)
-            else:
-                nc.vector.tensor_copy(out=dst, in_=src)
+            nc.vector.tensor_copy(
+                out=wg[:].rearrange("p (c i t) -> p c t i", i=4, t=4),
+                in_=w2raw[s][:].rearrange("p (t c i) -> p c t i", t=4, i=4),
+            )
             return wg
 
         def quant_w2(s, wg):
@@ -109,16 +113,21 @@ def tile_psicritic_pa_t_kernel(tc, h1, W2, b2, W3, b3, g1, V2, c2, V3, c3, out):
                 in_=wg[:],
             )
 
-        load_g(0)
+        load_g(0, 2)
         load_w2(3)
         nc.scalar.dma_start(out=bz[0 : 4 * A, :], in_=b2.rearrange("a (t p) -> (a t) p", p=P))
         nc.scalar.dma_start(out=bz[4 * A : 4 * NS, :], in_=c2.rearrange("(t p) -> t p", p=P))
         nc.scalar.dma_start(out=zrow[0:1, 0 : A * S], in_=b3.rearrange("(o a) s -> o (a s)", o=1))
         nc.scalar.dma_start(out=zrow[0:1, A * S :], in_=c3.rearrange("(o s) -> o s", o=1))
         load_h(0, False)
-        for a in range(A):
-            load_h_part(0, a)
-            load_w2(a)
+        load_h_part(0, 0)
+        load_w2(0)
+        load_h_part(0, 1)
+        load_w2(1)
+        load_h_part(0, 2)
+        load_g(1)
+        load_w2(2)
+        load_h(1, True)
         w3raw = const.tile([P, NS * 4 * S], BF16, name="w3raw")
         nc.sync.dma_start(
             out=w3raw[:, 0 : A * 4 * S].rearrange("p (x n) -> p x n", n=S),
@@ -128,9 +137,8 @@ def tile_psicritic_pa_t_kernel(tc, h1, W2, b2, W3, b3, g1, V2, c2, V3, c3, out):
             out=w3raw[:, A * 4 * S :].rearrange("p (x n) -> p x n", n=S),
             in_=V3.rearrange("(t p) n -> p t n", p=P),
         )
-        for r in (1, 2):
-            load_g(r)
-            load_h(r, True)
+        load_g(2)
+        load_h(2, True)
 
         xt = {}
         xq = {}
@@ -146,45 +154,52 @@ def tile_psicritic_pa_t_kernel(tc, h1, W2, b2, W3, b3, g1, V2, c2, V3, c3, out):
         def unit(u):
             return u // NS, ORDER[u % NS]
 
+        def halves(u):
+            return (chunks(u // NS) + 1) // 2
+
         def b_on_vector(u, hf):
-            return hf == 1 and u >= 2 and u % 2 == 0
+            return V_SHARE > 0 and hf == 1 and 2 <= u < 26 and u % V_SHARE == 0
 
         def st_a(u, hf):
             r, s = unit(u)
+            nj = min(2, chunks(r) - 2 * hf)
             x32 = (xg[r] if s == 3 else xh[r])[:].bitcast(F32)
             xt[u, hf] = ps_x.tile([P, 512], F32, name="xt", tag="xt")
             for uu in range(2):
-                for jj in range(2):
+                for jj in range(nj):
                     j = 2 * hf + jj
                     col = (j * 256 if s == 3 else (j * A + s) * 256) + 128 * uu
                     nc.tensor.transpose(
-                        xt[u, hf][:, (2 * uu + jj) * P : (2 * uu + jj + 1) * P],
+                        xt[u, hf][:, (nj * uu + jj) * P : (nj * uu + jj + 1) * P],
                         x32[:, col : col + P],
                         ident[:],
                     )
 
         def st_b(u, hf):
+            r, s = unit(u)
+            nj = min(2, chunks(r) - 2 * hf)
             if hf == 0:
-                xq[u] = xqp.tile([P, 4 * ROUND], BF16, name="xq", tag="xq", align_bytes=64)
-            dst = xq[u][:].bitcast(F32).rearrange("p (w u) -> p w u", u=2)[:, 256 * hf : 256 * (hf + 1), :]
-            src = xt[u, hf][:].rearrange("p (u w) -> p w u", u=2)
+                xq[u] = xqp.tile([P, 4 * ROUNDS[r]], BF16, name="xq", tag="xq", align_bytes=64)
+            dst = xq[u][:].bitcast(F32).rearrange("p (w u) -> p w u", u=2)[:, 256 * hf : 256 * hf + P * nj, :]
+            src = xt[u, hf][:, 0 : 2 * P * nj].rearrange("p (u w) -> p w u", u=2)
             if b_on_vector(u, hf):
                 nc.vector.tensor_copy(out=dst, in_=src)
             else:
                 nc.scalar.copy(out=dst, in_=src)
 
         def st_c(u):
-            codes = xqp.tile([P, ROUND], U32, name="xc", tag="xc", align_bytes=64)
-            scales = xqp.tile([P, ROUND], U8, name="xs", tag="xs", align_bytes=64)
+            n_tok = ROUNDS[u // NS]
+            codes = xqp.tile([P, n_tok], U32, name="xc", tag="xc", align_bytes=64)
+            scales = xqp.tile([P, n_tok], U8, name="xs", tag="xs", align_bytes=64)
             xc[u] = (codes, scales)
             nc.vector.quantize_mx(out=codes[:].bitcast(FP8X4), scales=scales[:], in_=xq[u][:])
 
         def st_d(u, t):
             r, s = unit(u)
-            hps[u, t] = ps_h.tile([P, ROUND], F32, name="hps", tag="hps")
+            hps[u, t] = ps_h.tile([P, 512], F32, name="hps", tag="hps")
             col = F * s + P * t
             nc.tensor.matmul_mx(
-                out=hps[u, t][:],
+                out=hps[u, t][:, 0 : ROUNDS[r]],
                 lhsT=w2c[:, col : col + P].bitcast(FP8X4),
                 lhsT_scale=w2s[:, col : col + P],
                 rhs=xc[u][0][:].bitcast(FP8X4),
@@ -195,40 +210,28 @@ def tile_psicritic_pa_t_kernel(tc, h1, W2, b2, W3, b3, g1, V2, c2, V3, c3, out):
 
         def st_e(u, t):
             r, s = unit(u)
+            n_tok = ROUNDS[r]
             if t == 0:
-                hp[u] = hpp.tile([P, 4 * ROUND], BF16, name="hp", tag="hp")
+                hp[u] = hpp.tile([P, 4 * n_tok], BF16, name="hp", tag="hp")
             nc.scalar.activation(
-                out=hp[u][:, ROUND * t : ROUND * (t + 1)],
-                in_=hps[u, t][:],
+                out=hp[u][:, n_tok * t : n_tok * (t + 1)],
+                in_=hps[u, t][:, 0:n_tok],
                 func=ACT.Relu,
                 bias=bias2[:, 4 * s + t : 4 * s + t + 1],
                 scale=1.0,
             )
 
         def st_f(u):
-            hq[u] = hpp.tile([P, 4 * ROUND], BF16, name="hq", tag="hq", align_bytes=64)
-            gcols = G_COLS if NS <= u < NU - 1 else 0
-            cut = ROUND - gcols
-            planes = hp[u][:].rearrange("p (t w) -> p t w", t=4)
+            hq[u] = hpp.tile([P, 4 * ROUNDS[u // NS]], BF16, name="hq", tag="hq", align_bytes=64)
             nc.vector.tensor_copy(
-                out=hq[u][:, 0 : 4 * cut].rearrange("p (c i t) -> p c t i", i=4, t=4),
-                in_=planes[:, :, 0:cut].rearrange("p t (c i) -> p c t i", i=4),
+                out=hq[u][:].rearrange("p (c i t) -> p c t i", i=4, t=4),
+                in_=hp[u][:].rearrange("p (t c i) -> p c t i", t=4, i=4),
             )
-            if gcols:
-                nc.gpsimd.tensor_copy(out=junk[:, 0:1], in_=hq[u][:, 0:1])
-                nc.gpsimd.tensor_scalar(
-                    out=hq[u][:, 4 * cut :].rearrange("p (c i t) -> p c t i", i=4, t=4),
-                    in0=planes[:, :, cut:].rearrange("p t (c i) -> p c t i", i=4),
-                    scalar1=1.0,
-                    scalar2=0.0,
-                    op0=ALU.mult,
-                    op1=ALU.add,
-                )
 
         def st_g(u):
             r, s = unit(u)
-            codes = hcp.tile([P, ROUND], U32, name="hc%d" % s, tag="hc%d" % s, align_bytes=64)
-            scales = hcp.tile([P, ROUND], U8, name="hs%d" % s, tag="hs%d" % s, align_bytes=64)
+            codes = hcp.tile([P, ROUNDS[r]], U32, name="hc%d" % s, tag="hc%d" % s, align_bytes=64)
+            scales = hcp.tile([P, ROUNDS[r]], U8, name="hs%d" % s, tag="hs%d" % s, align_bytes=64)
             hc[r, s] = (codes, scales)
             nc.vector.quantize_mx(out=codes[:].bitcast(FP8X4), scales=scales[:], in_=hq[u][:])
 
@@ -247,7 +250,7 @@ def tile_psicritic_pa_t_kernel(tc, h1, W2, b2, W3, b3, g1, V2, c2, V3, c3, out):
             ops[r, j] = ps_o.tile([P, 4 * S], F32, name="ops", tag="ops")
             for a in range(A):
                 dst = ops[r, j][:, S * a : S * (a + 1)]
-                if r < FULL_ROUNDS:
+                if r in FULL:
                     l2_pass(dst, r, 3, j, 3, True, False)
                     l2_pass(dst, r, 3, j, 7, False, False)
                     for b in range(A):
@@ -255,12 +258,12 @@ def tile_psicritic_pa_t_kernel(tc, h1, W2, b2, W3, b3, g1, V2, c2, V3, c3, out):
                 else:
                     l2_pass(dst, r, 3, j, 3, True, False)
                     l2_pass(dst, r, a, j, a, False, True)
-            if r >= FULL_ROUNDS:
+            if r not in FULL:
                 for a in range(A):
                     l2_pass(ops[r, j][:, S * A :], r, a, j, 4 + a, a == 0, a == A - 1)
 
         def st_i1(r, j):
-            if r < FULL_ROUNDS:
+            if r in FULL:
                 return
             esb[r, j] = outp.tile([P, A * S], F32, name="esb", tag="esb")
             nc.vector.scalar_tensor_tensor(
@@ -273,9 +276,10 @@ def tile_psicritic_pa_t_kernel(tc, h1, W2, b2, W3, b3, g1, V2, c2, V3, c3, out):
             )
 
         def st_i2(r, j):
+            nj = chunks(r)
             if j == 0:
-                osb[r] = outp.tile([P, 4 * A * S], F32, name="osb", tag="osb")
-            full = r < FULL_ROUNDS
+                osb[r] = outp.tile([P, nj * A * S], F32, name="osb", tag="osb")
+            full = r in FULL
             nc.vector.scalar_tensor_tensor(
                 out=osb[r][:, A * S * j : A * S * (j + 1)],
                 in0=ops[r, j][:, 0 : A * S],
@@ -284,14 +288,9 @@ def tile_psicritic_pa_t_kernel(tc, h1, W2, b2, W3, b3, g1, V2, c2, V3, c3, out):
                 op0=ALU.mult,
                 op1=ALU.add,
             )
-            rows = out[ROUND * r : ROUND * (r + 1)]
-            if r == NR - 1:
-                nc.sync.dma_start(
-                    out=rows.rearrange("(p j) a s -> p j (a s)", j=4)[:, j : j + 1, :],
-                    in_=osb[r][:, A * S * j : A * S * (j + 1)].unsqueeze(1),
-                )
-            elif j == 3:
-                nc.sync.dma_start(out=rows.rearrange("(p j) a s -> p (j a s)", j=4), in_=osb[r][:])
+            if j == nj - 1:
+                rows = out[base[r] : base[r] + ROUNDS[r]]
+                nc.sync.dma_start(out=rows.rearrange("(p j) a s -> p (j a s)", j=nj), in_=osb[r][:])
 
         def setup_bias2():
             bz32 = const.tile([P, P], F32, name="bz32")
@@ -341,12 +340,15 @@ def tile_psicritic_pa_t_kernel(tc, h1, W2, b2, W3, b3, g1, V2, c2, V3, c3, out):
         ready = []
         h_done = []
         seen = {}
+        n_chunks = B // P
 
         def b_unit(u):
+            nxt = state["a"]
             for hf in range(2):
-                st_b(u, hf)
-                if state["a"] < NU:
-                    st_a(state["a"], hf)
+                if hf < halves(u):
+                    st_b(u, hf)
+                if nxt < NU and hf < halves(nxt):
+                    st_a(nxt, hf)
             state["a"] += 1
             state["b"] = u + 1
 
@@ -355,7 +357,7 @@ def tile_psicritic_pa_t_kernel(tc, h1, W2, b2, W3, b3, g1, V2, c2, V3, c3, out):
             r = u // NS
             seen[r] = seen.get(r, 0) + 1
             if seen[r] == NS:
-                for j in range(4):
+                for j in range(chunks(r)):
                     ready.append((r, j, n))
 
         def try_h(n, force):
@@ -382,7 +384,7 @@ def tile_psicritic_pa_t_kernel(tc, h1, W2, b2, W3, b3, g1, V2, c2, V3, c3, out):
             st_d(0, t)
         pending = {0: prep_w2(0)}
         b_unit(1)
-        for n in range(NU + 2):
+        for n in range(NU + 1):
             if n >= 2 and n % NS == 2 and n // NS + 3 < NR:
                 load_g(n // NS + 3)
                 load_h(n // NS + 3, True)
@@ -403,26 +405,27 @@ def tile_psicritic_pa_t_kernel(tc, h1, W2, b2, W3, b3, g1, V2, c2, V3, c3, out):
                 setup_beta()
             if n == 4:
                 nc.vector.quantize_mx(out=w3c[:].bitcast(FP8X4), scales=w3s[:], in_=pending[3][:])
-            chunk = pop_i(n, n >= NU)
+            late = n >= NU - 2 * NS
+            chunk = pop_i(n, late)
             if n < NU:
                 for t in range(4):
                     st_e(n, t)
                     if n + 1 < NU:
                         st_d(n + 1, t)
-            try_h(n, n >= NU)
-            if 2 <= n:
-                quantise_h(n - 2, n)
-            if 1 <= n <= NU:
+            try_h(n, late)
+            if n >= 1:
                 st_f(n - 1)
-            if chunk:
-                st_i1(chunk[0], chunk[1])
             count = 0
-            while state["b"] < NU and state["b"] <= n + (2 if n < 1 else LEAD_B) and count < 2:
+            while state["b"] < NU and state["b"] <= n + (2 if n < 3 else LEAD_B) and count < 2:
                 b_unit(state["b"])
                 count += 1
             if chunk:
+                st_i1(chunk[0], chunk[1])
+            if n >= 1:
+                quantise_h(n - 1, n)
+            if chunk:
                 st_i2(chunk[0], chunk[1])
-        while state["i"] < NR * 4:
+        while state["i"] < n_chunks:
             try_h(NU, True)
             try_h(NU, True)
             while state["i"] < len(h_done):

@@ -22,8 +22,8 @@ FLOPS = 2 * NS * B * (F * F + F * S)
 
 LEAD_B = 3
 LEAD_C = 2
-FULL = (0, 1, 2, 3, 4, 5, 6)
-V_SHARE = 6
+FULL = ()
+V_SHARE = 3
 
 
 def tile_psicritic_pa_t_kernel(tc, h1, W2, b2, W3, b3, g1, V2, c2, V3, c3, out):
@@ -158,7 +158,7 @@ def tile_psicritic_pa_t_kernel(tc, h1, W2, b2, W3, b3, g1, V2, c2, V3, c3, out):
             return (chunks(u // NS) + 1) // 2
 
         def b_on_vector(u, hf):
-            return V_SHARE > 0 and hf == 1 and 2 <= u < 26 and u % V_SHARE == 0
+            return V_SHARE > 0 and hf == 1 and 2 <= u < 28 and u % V_SHARE == 0
 
         def st_a(u, hf):
             r, s = unit(u)

@@ -22,8 +22,8 @@ FLOPS = 2 * NS * B * (F * F + F * S)
 
 LEAD_B = 3
 LEAD_C = 2
-FULL = ()
-V_SHARE = 3
+FULL_EVERY = 2
+V_SHARE = 2
 
 
 def tile_psicritic_pa_t_kernel(tc, h1, W2, b2, W3, b3, g1, V2, c2, V3, c3, out):
@@ -63,6 +63,9 @@ def tile_psicritic_pa_t_kernel(tc, h1, W2, b2, W3, b3, g1, V2, c2, V3, c3, out):
         def chunks(r):
             return ROUNDS[r] // P
 
+        def is_full(r, j):
+            return ROUNDS[r] == 512 and j % FULL_EVERY == 0
+
         def load_g(r, parts=1):
             nj = chunks(r)
             xg[r] = xin.tile([P, nj * F], BF16, name="xg", tag="xg")
@@ -100,10 +103,9 @@ def tile_psicritic_pa_t_kernel(tc, h1, W2, b2, W3, b3, g1, V2, c2, V3, c3, out):
 
         def prep_w2(s):
             wg = wst.tile([P, 4 * F], BF16, name="wg", tag="wg", align_bytes=64)
-            nc.vector.tensor_copy(
-                out=wg[:].rearrange("p (c i t) -> p c t i", i=4, t=4),
-                in_=w2raw[s][:].rearrange("p (t c i) -> p c t i", t=4, i=4),
-            )
+            dst = wg[:].rearrange("p (c i t) -> p c t i", i=4, t=4)
+            src = w2raw[s][:].rearrange("p (t c i) -> p c t i", t=4, i=4)
+            nc.vector.tensor_copy(out=dst, in_=src)
             return wg
 
         def quant_w2(s, wg):
@@ -158,7 +160,7 @@ def tile_psicritic_pa_t_kernel(tc, h1, W2, b2, W3, b3, g1, V2, c2, V3, c3, out):
             return (chunks(u // NS) + 1) // 2
 
         def b_on_vector(u, hf):
-            return V_SHARE > 0 and hf == 1 and 2 <= u < 28 and u % V_SHARE == 0
+            return V_SHARE > 0 and hf == 1 and 2 <= u < 26 and u % V_SHARE == 0
 
         def st_a(u, hf):
             r, s = unit(u)
@@ -250,7 +252,7 @@ def tile_psicritic_pa_t_kernel(tc, h1, W2, b2, W3, b3, g1, V2, c2, V3, c3, out):
             ops[r, j] = ps_o.tile([P, 4 * S], F32, name="ops", tag="ops")
             for a in range(A):
                 dst = ops[r, j][:, S * a : S * (a + 1)]
-                if r in FULL:
+                if is_full(r, j):
                     l2_pass(dst, r, 3, j, 3, True, False)
                     l2_pass(dst, r, 3, j, 7, False, False)
                     for b in range(A):
@@ -258,12 +260,12 @@ def tile_psicritic_pa_t_kernel(tc, h1, W2, b2, W3, b3, g1, V2, c2, V3, c3, out):
                 else:
                     l2_pass(dst, r, 3, j, 3, True, False)
                     l2_pass(dst, r, a, j, a, False, True)
-            if r not in FULL:
+            if not is_full(r, j):
                 for a in range(A):
                     l2_pass(ops[r, j][:, S * A :], r, a, j, 4 + a, a == 0, a == A - 1)
 
         def st_i1(r, j):
-            if r in FULL:
+            if is_full(r, j):
                 return
             esb[r, j] = outp.tile([P, A * S], F32, name="esb", tag="esb")
             nc.vector.scalar_tensor_tensor(
@@ -279,7 +281,7 @@ def tile_psicritic_pa_t_kernel(tc, h1, W2, b2, W3, b3, g1, V2, c2, V3, c3, out):
             nj = chunks(r)
             if j == 0:
                 osb[r] = outp.tile([P, nj * A * S], F32, name="osb", tag="osb")
-            full = r in FULL
+            full = is_full(r, j)
             nc.vector.scalar_tensor_tensor(
                 out=osb[r][:, A * S * j : A * S * (j + 1)],
                 in0=ops[r, j][:, 0 : A * S],

@@ -64,7 +64,7 @@ def tile_psicritic_pa_t_kernel(tc, h1, W2, b2, W3, b3, g1, V2, c2, V3, c3, out):
             return ROUNDS[r] // P
 
         def is_full(r, j):
-            return ROUNDS[r] == 512 and j % FULL_EVERY == 0
+            return ROUNDS[r] == 512 and j % 4 != 3
 
         def load_g(r, parts=1):
             nj = chunks(r)
@@ -160,7 +160,7 @@ def tile_psicritic_pa_t_kernel(tc, h1, W2, b2, W3, b3, g1, V2, c2, V3, c3, out):
             return (chunks(u // NS) + 1) // 2
 
         def b_on_vector(u, hf):
-            return V_SHARE > 0 and hf == 1 and 2 <= u < 26 and u % V_SHARE == 0
+            return V_SHARE > 0 and hf == 1 and 2 <= u < 28 and u % V_SHARE == 0
 
         def st_a(u, hf):
             r, s = unit(u)

@@ -45,6 +45,8 @@ def tile_psicritic_pa_t_kernel(tc, h1, W2, b2, W3, b3, g1, V2, c2, V3, c3, out):
         make_identity(nc, ident[:])
         ones = const.tile([P, P], BF16, name="ones")
         nc.vector.memset(ones[:], 1.0)
+        warm = const.tile([P, 16], BF16, name="warm")
+        nc.scalar.activation(out=warm[:, 0:1], in_=ones[:, 0:1], func=ACT.Relu)
         bz = const.tile([P, P], BF16, name="bz")
         nc.vector.memset(bz[:], 0.0)
         zrow = const.tile([P, 4 * S], BF16, name="zrow")
@@ -64,7 +66,7 @@ def tile_psicritic_pa_t_kernel(tc, h1, W2, b2, W3, b3, g1, V2, c2, V3, c3, out):
             return ROUNDS[r] // P
 
         def is_full(r, j):
-            return ROUNDS[r] == 512 and j % 4 != 3
+            return ROUNDS[r] == 512 and (j < 2 or (j == 2 and r < 4))
 
         def load_g(r, parts=1):
             nj = chunks(r)
@@ -160,7 +162,7 @@ def tile_psicritic_pa_t_kernel(tc, h1, W2, b2, W3, b3, g1, V2, c2, V3, c3, out):
             return (chunks(u // NS) + 1) // 2
 
         def b_on_vector(u, hf):
-            return V_SHARE > 0 and hf == 1 and 2 <= u < 28 and u % V_SHARE == 0
+            return V_SHARE > 0 and hf == 1 and 2 <= u < 26 and u % V_SHARE == 0
 
         def st_a(u, hf):
             r, s = unit(u)

from contextlib import ExitStack

import concourse.mybir as mybir
from concourse.masks import make_identity

F32 = mybir.dt.float32
BF16 = mybir.dt.bfloat16
U32 = mybir.dt.uint32
U8 = mybir.dt.uint8
FP8X4 = mybir.dt.float8_e4m3fn_x4
ACT = mybir.ActivationFunctionType
ALU = mybir.AluOpType

P = 128
B, A, S, F = 4096, 3, 128, 512
NS = A + 1
ORDER = (3, 0, 1, 2)
ROUNDS = (512, 512, 512, 512, 512, 512, 512, 256, 256)
NR = len(ROUNDS)
NU = NR * NS
FLOPS = 2 * NS * B * (F * F + F * S)

LEAD_B = 3
LEAD_C = 2
FULL_EVERY = 2
V_SHARE = 2


def tile_psicritic_pa_t_kernel(tc, h1, W2, b2, W3, b3, g1, V2, c2, V3, c3, out):
    nc = tc.nc
    base = [sum(ROUNDS[:r]) for r in range(NR)]
    with ExitStack() as ctx:
        const = ctx.enter_context(tc.tile_pool(name="const", bufs=1))
        wst = ctx.enter_context(tc.tile_pool(name="wst", bufs=2))
        xin = ctx.enter_context(tc.tile_pool(name="xin", bufs=3))
        xqp = ctx.enter_context(tc.tile_pool(name="xqp", bufs=4))
        hpp = ctx.enter_context(tc.tile_pool(name="hpp", bufs=3))
        hcp = ctx.enter_context(tc.tile_pool(name="hcp", bufs=2))
        outp = ctx.enter_context(tc.tile_pool(name="outp", bufs=2))
        ps_x = ctx.enter_context(tc.psum_pool(name="ps_x", bufs=2))
        ps_h = ctx.enter_context(tc.psum_pool(name="ps_h", bufs=4))
        ps_o = ctx.enter_context(tc.psum_pool(name="ps_o", bufs=2))

        ident = const.tile([P, P], F32, name="ident")
        make_identity(nc, ident[:])
        ones = const.tile([P, P], BF16, name="ones")
        nc.vector.memset(ones[:], 1.0)
        warm = const.tile([P, 16], BF16, name="warm")
        nc.scalar.activation(out=warm[:, 0:1], in_=ones[:, 0:1], func=ACT.Relu)
        bz = const.tile([P, P], BF16, name="bz")
        nc.vector.memset(bz[:], 0.0)
        zrow = const.tile([P, 4 * S], BF16, name="zrow")
        nc.vector.memset(zrow[:], 0.0)

        w2c = const.tile([P, NS * F], U32, name="w2c", align_bytes=64)
        w2s = const.tile([P, NS * F], U8, name="w2s", align_bytes=64)
        w3c = const.tile([P, 8 * S], U32, name="w3c", align_bytes=64)
        w3s = const.tile([P, 8 * S], U8, name="w3s", align_bytes=64)
        bias2 = const.tile([P, 4 * NS], F32, name="bias2")
        beta = const.tile([P, A * S], F32, name="beta")

        xh = {}
        xg = {}

        def chunks(r):
            return ROUNDS[r] // P

        def is_full(r, j):
            return ROUNDS[r] == 512 and (j < 2 or (j == 2 and r < 4))

        def load_g(r, parts=1):
            nj = chunks(r)
            xg[r] = xin.tile([P, nj * F], BF16, name="xg", tag="xg")
            rows = g1[base[r] : base[r] + ROUNDS[r], :].rearrange("(p j) k -> p j k", j=nj)
            step = nj // parts
            for i in range(parts):
                nc.sync.dma_start(
                    out=xg[r][:, F * step * i : F * step * (i + 1)].rearrange("p (j k) -> p j k", k=F),
                    in_=rows[:, step * i : step * (i + 1), :],
                )

        def load_h(r, whole):
            nj = chunks(r)
            xh[r] = xin.tile([P, nj * A * F], BF16, name="xh", tag="xh")
            if whole:
                rows = h1[base[r] : base[r] + ROUNDS[r]]
                nc.sync.dma_start(out=xh[r][:], in_=rows.rearrange("(p j) a k -> p (j a k)", j=nj))

        def load_h_part(r, a):
            nj = chunks(r)
            rows = h1[base[r] : base[r] + ROUNDS[r], a : a + 1, :]
            nc.sync.dma_start(
                out=xh[r][:].rearrange("p (j a k) -> p j a k", j=nj, a=A)[:, :, a : a + 1, :],
                in_=rows.rearrange("(p j) o k -> p j o k", j=nj),
            )

        w2raw = {}

        def load_w2(s):
            w2raw[s] = wst.tile([P, 4 * F], BF16, name="w2raw", tag="w2raw", bufs=4)
            src = V2.rearrange("(u p e) n -> p u (e n)", u=2, e=2) if s == 3 else W2[
                s : s + 1
            ].rearrange("o (u p e) n -> p (o u) (e n)", u=2, e=2)
            nc.sync.dma_start(out=w2raw[s][:].rearrange("p (u x) -> p u x", u=2), in_=src)

        def prep_w2(s):
            wg = wst.tile([P, 4 * F], BF16, name="wg", tag="wg", align_bytes=64)
            dst = wg[:].rearrange("p (c i t) -> p c t i", i=4, t=4)
            src = w2raw[s][:].rearrange("p (t c i) -> p c t i", t=4, i=4)
            nc.vector.tensor_copy(out=dst, in_=src)
            return wg

        def quant_w2(s, wg):
            nc.vector.quantize_mx(
                out=w2c[:, F * s : F * (s + 1)].bitcast(FP8X4),
                scales=w2s[:, F * s : F * (s + 1)],
                in_=wg[:],
            )

        load_g(0, 2)
        load_w2(3)
        nc.scalar.dma_start(out=bz[0 : 4 * A, :], in_=b2.rearrange("a (t p) -> (a t) p", p=P))
        nc.scalar.dma_start(out=bz[4 * A : 4 * NS, :], in_=c2.rearrange("(t p) -> t p", p=P))
        nc.scalar.dma_start(out=zrow[0:1, 0 : A * S], in_=b3.rearrange("(o a) s -> o (a s)", o=1))
        nc.scalar.dma_start(out=zrow[0:1, A * S :], in_=c3.rearrange("(o s) -> o s", o=1))
        load_h(0, False)
        load_h_part(0, 0)
        load_w2(0)
        load_h_part(0, 1)
        load_w2(1)
        load_h_part(0, 2)
        load_g(1)
        load_w2(2)
        load_h(1, True)
        w3raw = const.tile([P, NS * 4 * S], BF16, name="w3raw")
        nc.sync.dma_start(
            out=w3raw[:, 0 : A * 4 * S].rearrange("p (x n) -> p x n", n=S),
            in_=W3.rearrange("a (t p) n -> p (a t) n", p=P),
        )
        nc.sync.dma_start(
            out=w3raw[:, A * 4 * S :].rearrange("p (x n) -> p x n", n=S),
            in_=V3.rearrange("(t p) n -> p t n", p=P),
        )
        load_g(2)
        load_h(2, True)

        xt = {}
        xq = {}
        xc = {}
        hps = {}
        hp = {}
        hq = {}
        hc = {}
        ops = {}
        osb = {}
        esb = {}

        def unit(u):
            return u // NS, ORDER[u % NS]

        def halves(u):
            return (chunks(u // NS) + 1) // 2

        def b_on_vector(u, hf):
            return V_SHARE > 0 and hf == 1 and 2 <= u < 26 and u % V_SHARE == 0

        def st_a(u, hf):
            r, s = unit(u)
            nj = min(2, chunks(r) - 2 * hf)
            x32 = (xg[r] if s == 3 else xh[r])[:].bitcast(F32)
            xt[u, hf] = ps_x.tile([P, 512], F32, name="xt", tag="xt")
            for uu in range(2):
                for jj in range(nj):
                    j = 2 * hf + jj
                    col = (j * 256 if s == 3 else (j * A + s) * 256) + 128 * uu
                    nc.tensor.transpose(
                        xt[u, hf][:, (nj * uu + jj) * P : (nj * uu + jj + 1) * P],
                        x32[:, col : col + P],
                        ident[:],
                    )

        def st_b(u, hf):
            r, s = unit(u)
            nj = min(2, chunks(r) - 2 * hf)
            if hf == 0:
                xq[u] = xqp.tile([P, 4 * ROUNDS[r]], BF16, name="xq", tag="xq", align_bytes=64)
            dst = xq[u][:].bitcast(F32).rearrange("p (w u) -> p w u", u=2)[:, 256 * hf : 256 * hf + P * nj, :]
            src = xt[u, hf][:, 0 : 2 * P * nj].rearrange("p (u w) -> p w u", u=2)
            if b_on_vector(u, hf):
                nc.vector.tensor_copy(out=dst, in_=src)
            else:
                nc.scalar.copy(out=dst, in_=src)

        def st_c(u):
            n_tok = ROUNDS[u // NS]
            codes = xqp.tile([P, n_tok], U32, name="xc", tag="xc", align_bytes=64)
            scales = xqp.tile([P, n_tok], U8, name="xs", tag="xs", align_bytes=64)
            xc[u] = (codes, scales)
            nc.vector.quantize_mx(out=codes[:].bitcast(FP8X4), scales=scales[:], in_=xq[u][:])

        def st_d(u, t):
            r, s = unit(u)
            hps[u, t] = ps_h.tile([P, 512], F32, name="hps", tag="hps")
            col = F * s + P * t
            nc.tensor.matmul_mx(
                out=hps[u, t][:, 0 : ROUNDS[r]],
                lhsT=w2c[:, col : col + P].bitcast(FP8X4),
                lhsT_scale=w2s[:, col : col + P],
                rhs=xc[u][0][:].bitcast(FP8X4),
                rhs_scale=xc[u][1][:],
                start=True,
                stop=True,
            )

        def st_e(u, t):
            r, s = unit(u)
            n_tok = ROUNDS[r]
            if t == 0:
                hp[u] = hpp.tile([P, 4 * n_tok], BF16, name="hp", tag="hp")
            nc.scalar.activation(
                out=hp[u][:, n_tok * t : n_tok * (t + 1)],
                in_=hps[u, t][:, 0:n_tok],
                func=ACT.Relu,
                bias=bias2[:, 4 * s + t : 4 * s + t + 1],
                scale=1.0,
            )

        def st_f(u):
            hq[u] = hpp.tile([P, 4 * ROUNDS[u // NS]], BF16, name="hq", tag="hq", align_bytes=64)
            nc.vector.tensor_copy(
                out=hq[u][:].rearrange("p (c i t) -> p c t i", i=4, t=4),
                in_=hp[u][:].rearrange("p (t c i) -> p c t i", t=4, i=4),
            )

        def st_g(u):
            r, s = unit(u)
            codes = hcp.tile([P, ROUNDS[r]], U32, name="hc%d" % s, tag="hc%d" % s, align_bytes=64)
            scales = hcp.tile([P, ROUNDS[r]], U8, name="hs%d" % s, tag="hs%d" % s, align_bytes=64)
            hc[r, s] = (codes, scales)
            nc.vector.quantize_mx(out=codes[:].bitcast(FP8X4), scales=scales[:], in_=hq[u][:])

        def l2_pass(dst, r, s, j, blk, start, stop):
            nc.tensor.matmul_mx(
                out=dst,
                lhsT=hc[r, s][0][:, P * j : P * (j + 1)].bitcast(FP8X4),
                lhsT_scale=hc[r, s][1][:, P * j : P * (j + 1)],
                rhs=w3c[:, S * blk : S * (blk + 1)].bitcast(FP8X4),
                rhs_scale=w3s[:, S * blk : S * (blk + 1)],
                start=start,
                stop=stop,
            )

        def st_h(r, j):
            ops[r, j] = ps_o.tile([P, 4 * S], F32, name="ops", tag="ops")
            for a in range(A):
                dst = ops[r, j][:, S * a : S * (a + 1)]
                if is_full(r, j):
                    l2_pass(dst, r, 3, j, 3, True, False)
                    l2_pass(dst, r, 3, j, 7, False, False)
                    for b in range(A):
                        l2_pass(dst, r, b, j, b if b == a else 4 + b, False, b == A - 1)
                else:
                    l2_pass(dst, r, 3, j, 3, True, False)
                    l2_pass(dst, r, a, j, a, False, True)
            if not is_full(r, j):
                for a in range(A):
                    l2_pass(ops[r, j][:, S * A :], r, a, j, 4 + a, a == 0, a == A - 1)

        def st_i1(r, j):
            if is_full(r, j):
                return
            esb[r, j] = outp.tile([P, A * S], F32, name="esb", tag="esb")
            nc.vector.scalar_tensor_tensor(
                out=esb[r, j][:].rearrange("p (a s) -> p a s", a=A),
                in0=ops[r, j][:, S * A :].unsqueeze(1).to_broadcast([P, A, S]),
                scalar=1.0 / 3.0,
                in1=beta[:].rearrange("p (a s) -> p a s", a=A),
                op0=ALU.mult,
                op1=ALU.add,
            )

        def st_i2(r, j):
            nj = chunks(r)
            if j == 0:
                osb[r] = outp.tile([P, nj * A * S], F32, name="osb", tag="osb")
            full = is_full(r, j)
            nc.vector.scalar_tensor_tensor(
                out=osb[r][:, A * S * j : A * S * (j + 1)],
                in0=ops[r, j][:, 0 : A * S],
                scalar=1.0 / 3.0 if full else 0.5,
                in1=beta[:] if full else esb[r, j][:],
                op0=ALU.mult,
                op1=ALU.add,
            )
            if j == nj - 1:
                rows = out[base[r] : base[r] + ROUNDS[r]]
                nc.sync.dma_start(out=rows.rearrange("(p j) a s -> p (j a s)", j=nj), in_=osb[r][:])

        def setup_bias2():
            bz32 = const.tile([P, P], F32, name="bz32")
            nc.vector.tensor_copy(out=bz32[:], in_=bz[:])
            pt = ps_o.tile([P, 4 * S], F32, name="pt", tag="ops")
            nc.tensor.transpose(pt[:, 0:P], bz32[:], ident[:])
            wg = prep_w2(3)
            nc.vector.tensor_copy(out=bias2[:], in_=pt[:, 0 : 4 * NS])
            quant_w2(3, wg)

        def setup_beta():
            pb = ps_o.tile([P, 4 * S], F32, name="pb", tag="ops")
            nc.tensor.matmul(out=pb[:], lhsT=ones[:], rhs=zrow[:], start=True, stop=True)
            bb = const.tile([P, 4 * S], F32, name="bb")
            nc.vector.tensor_copy(out=bb[:], in_=pb[:])
            m1 = const.tile([P, S], F32, name="m1")
            nc.vector.tensor_tensor(out=m1[:], in0=bb[:, 0:S], in1=bb[:, S : 2 * S], op=ALU.add)
            m2 = const.tile([P, S], F32, name="m2")
            nc.vector.tensor_tensor(out=m2[:], in0=m1[:], in1=bb[:, 2 * S : 3 * S], op=ALU.add)
            gm = const.tile([P, S], F32, name="gm")
            nc.vector.scalar_tensor_tensor(
                out=gm[:], in0=m2[:], scalar=-1.0 / 3.0, in1=bb[:, 3 * S :], op0=ALU.mult, op1=ALU.add
            )
            nc.vector.tensor_tensor(
                out=beta[:].rearrange("p (a s) -> p a s", a=A),
                in0=bb[:, 0 : A * S].rearrange("p (a s) -> p a s", a=A),
                in1=gm[:].unsqueeze(1).to_broadcast([P, A, S]),
                op=ALU.add,
            )

        def setup_w3():
            w3g = const.tile([P, 8 * 4 * S], BF16, name="w3g", align_bytes=64)
            for lo, hi, src_lo, factor in ((0, 4, 0, 2.0), (4, 7, 0, -1.0), (7, 8, 3, 1.0)):
                nc.gpsimd.tensor_scalar(
                    out=w3g[:, 4 * S * lo : 4 * S * hi].rearrange("p (s n t) -> p s n t", s=hi - lo, t=4),
                    in0=w3raw[:, 4 * S * src_lo : 4 * S * (src_lo + hi - lo)].rearrange(
                        "p (s t n) -> p s n t", s=hi - lo, t=4
                    ),
                    scalar1=factor,
                    scalar2=0.0,
                    op0=ALU.mult,
                    op1=ALU.add,
                )
            return w3g

        state = {"a": 0, "b": 0, "c": 0, "h": 0, "i": 0}
        ready = []
        h_done = []
        seen = {}
        n_chunks = B // P

        def b_unit(u):
            nxt = state["a"]
            for hf in range(2):
                if hf < halves(u):
                    st_b(u, hf)
                if nxt < NU and hf < halves(nxt):
                    st_a(nxt, hf)
            state["a"] += 1
            state["b"] = u + 1

        def quantise_h(u, n):
            st_g(u)
            r = u // NS
            seen[r] = seen.get(r, 0) + 1
            if seen[r] == NS:
                for j in range(chunks(r)):
                    ready.append((r, j, n))

        def try_h(n, force):
            if state["h"] < len(ready) and (force or ready[state["h"]][2] <= n - 1):
                r, j = ready[state["h"]][0:2]
                state["h"] += 1
                st_h(r, j)
                h_done.append((r, j, n))

        def pop_i(n, force):
            if state["i"] < len(h_done) and (force or h_done[state["i"]][2] <= n - 1):
                state["i"] += 1
                return h_done[state["i"] - 1]
            return None

        st_a(0, 0)
        st_a(0, 1)
        state["a"] = 1
        setup_bias2()
        b_unit(0)
        st_c(0)
        state["c"] = 1
        for t in range(4):
            st_d(0, t)
        pending = {0: prep_w2(0)}
        b_unit(1)
        for n in range(NU + 1):
            if n >= 2 and n % NS == 2 and n // NS + 3 < NR:
                load_g(n // NS + 3)
                load_h(n // NS + 3, True)
            while state["c"] < NU and state["c"] <= n + LEAD_C and state["c"] < state["b"]:
                st_c(state["c"])
                state["c"] += 1
                if n < 2:
                    break
            if n == 0:
                quant_w2(0, pending[0])
                pending[1] = prep_w2(1)
            if n == 1:
                quant_w2(1, pending[1])
                pending[2] = prep_w2(2)
            if n == 2:
                quant_w2(2, pending[2])
                pending[3] = setup_w3()
                setup_beta()
            if n == 4:
                nc.vector.quantize_mx(out=w3c[:].bitcast(FP8X4), scales=w3s[:], in_=pending[3][:])
            late = n >= NU - 2 * NS
            chunk = pop_i(n, late)
            if n < NU:
                for t in range(4):
                    st_e(n, t)
                    if n + 1 < NU:
                        st_d(n + 1, t)
            try_h(n, late)
            if n >= 1:
                st_f(n - 1)
            count = 0
            while state["b"] < NU and state["b"] <= n + (2 if n < 3 else LEAD_B) and count < 2:
                b_unit(state["b"])
                count += 1
            if chunk:
                st_i1(chunk[0], chunk[1])
            if n >= 1:
                quantise_h(n - 1, n)
            if chunk:
                st_i2(chunk[0], chunk[1])
        while state["i"] < n_chunks:
            try_h(NU, True)
            try_h(NU, True)
            while state["i"] < len(h_done):
                chunk = pop_i(NU, True)
                st_i1(chunk[0], chunk[1])
                st_i2(chunk[0], chunk[1])
